import numpy as np
import ml_dtypes

BF16 = ml_dtypes.bfloat16


def bf(x):
    return np.asarray(x, np.float32).astype(BF16)


def f32(x):
    return np.asarray(x, np.float32)


def f64(x):
    return np.asarray(x).astype(np.float64)


def striped(idx):
    return np.tile(idx.reshape(-1, 16).T, (8, 1))


D, K, C, S, N = 128, 256, 256, 256, 128
NEAR = 24.0


def setup_inputs():
    return {"x": bf(1.5 * np.random.standard_normal((D, N))), "x_neighbors": bf(1.5 * np.random.standard_normal((D, K))), "y": bf(2.0 * np.random.standard_normal((K, C))), "base": f32(0.3 * np.random.standard_normal((C, S))), "offs": striped(np.random.permutation(S)[:N])}


def reference(x, x_neighbors, y, base, offs):
    idx = offs[:16].T.reshape(-1)
    q = f64(x)
    nb = f64(x_neighbors)
    a_sq = np.sum(q * q, axis=0)[None, :]
    b_sq = np.sum(nb * nb, axis=0)[:, None]
    d2 = a_sq + b_sq - 2.0 * (nb.T @ q)
    e = np.exp(NEAR - np.sqrt(d2))
    num = f64(y).T @ e
    rden = 1.0 / np.sum(e, axis=0)[None, :]
    res = f64(base).copy()
    res[:, idx] = num * rden
    return res

@@ -1,0 +1,80 @@
+import concourse.mybir as mybir
+
+BF16 = mybir.dt.bfloat16
+F32 = mybir.dt.float32
+U16 = mybir.dt.uint16
+ACT = mybir.ActivationFunctionType
+ALU = mybir.AluOpType
+
+P = 128
+D, K, C, S, N = 128, 256, 256, 256, 128
+KB = K // P
+CB = C // P
+NEAR = 24.0
+D2_FLOOR = 1e-18
+FLOPS = 2 * D * K * N + 2 * K * C * N
+
+
+def tile_nona_kernel(tc, x, x_neighbors, y, base, offs, out):
+    nc = tc.nc
+    y_blocks = y.rearrange("(b p) c -> b p c", p=P)
+    base_blocks = base.rearrange("(b p) s -> b p s", p=P)
+    out_blocks = out.rearrange("(b p) s -> b p s", p=P)
+
+    with tc.tile_pool(name="held", bufs=1) as held, tc.psum_pool(name="psum", bufs=1) as psum:
+        nb_sb = held.tile([P, K], BF16, name="nb_sb")
+        nc.sync.dma_start(nb_sb[:], x_neighbors)
+        x_sb = held.tile([P, N], BF16, name="x_sb")
+        nc.scalar.dma_start(x_sb[:], x)
+        offsets = held.tile([P, N // 16], U16, name="offsets")
+        nc.sync.dma_start(offsets[:], offs)
+        y_sb = [held.tile([P, C], BF16, name=f"y_sb{kb}") for kb in range(KB)]
+        for kb in range(KB):
+            nc.sync.dma_start(y_sb[kb][:], y_blocks[kb, :, :])
+        window = [held.tile([P, S], F32, name=f"window{cb}") for cb in range(CB)]
+        for cb in range(CB):
+            nc.scalar.dma_start(window[cb][:], base_blocks[cb, :, :])
+
+        neg_half = held.tile([P, P], BF16, name="neg_half")
+        nc.gpsimd.memset(neg_half[:], -0.5)
+        ones = held.tile([P, P], BF16, name="ones")
+        nc.gpsimd.memset(ones[:], 1.0)
+        near = held.tile([P, 1], F32, name="near")
+        nc.gpsimd.memset(near[:], NEAR)
+
+        nb_sq = held.tile([P, K], BF16, name="nb_sq")
+        nc.vector.tensor_tensor(nb_sq[:], nb_sb[:], nb_sb[:], ALU.mult)
+        x_sq = held.tile([P, N], BF16, name="x_sq")
+        nc.vector.tensor_tensor(x_sq[:], x_sb[:], x_sb[:], ALU.mult)
+        neg_half_d2 = [psum.tile([P, N], F32, name=f"neg_half_d2_{kb}") for kb in range(KB)]
+        for kb in range(KB):
+            nc.tensor.matmul(neg_half_d2[kb][:], nb_sb[:, kb * P : (kb + 1) * P], x_sb[:], start=True, stop=False)
+        for kb in range(KB):
+            nc.tensor.matmul(neg_half_d2[kb][:], nb_sq[:, kb * P : (kb + 1) * P], neg_half[:], start=False, stop=False)
+            nc.tensor.matmul(neg_half_d2[kb][:], neg_half[:], x_sq[:], start=False, stop=True)
+
+        e = [held.tile([P, N], BF16, name=f"e{kb}") for kb in range(KB)]
+        dist = [held.tile([P, N], F32, name=f"dist{kb}") for kb in range(KB)]
+        for kb in range(KB):
+            d2 = held.tile([P, N], F32, name=f"d2_{kb}")
+            nc.vector.tensor_scalar(d2[:], neg_half_d2[kb][:], -2.0, D2_FLOOR, ALU.mult, ALU.max)
+            nc.scalar.activation(dist[kb][:], d2[:], ACT.Sqrt)
+        for kb in range(KB):
+            nc.scalar.activation(e[kb][:], dist[kb][:], ACT.Exp, bias=near[:], scale=-1.0)
+
+        den = psum.tile([P, N], F32, name="den")
+        num = [psum.tile([P, N], F32, name=f"num{cb}") for cb in range(CB)]
+        for kb in range(KB):
+            first, last = kb == 0, kb == KB - 1
+            nc.tensor.matmul(den[:], ones[:], e[kb][:], start=first, stop=last)
+            for cb in range(CB):
+                nc.tensor.matmul(num[cb][:], y_sb[kb][:, cb * P : (cb + 1) * P], e[kb][:], start=first, stop=last)
+        rden = held.tile([P, N], F32, name="rden")
+        nc.vector.reciprocal(rden[:], den[:])
+        num_sb = [held.tile([P, N], F32, name=f"num_sb{cb}") for cb in range(CB)]
+        for cb in range(CB):
+            nc.scalar.copy(num_sb[cb][:], num[cb][:])
+
+        for cb in range(CB):
+            nc.vector.tensor_tensor(window[cb][:].indirect(offsets[:]), num_sb[cb][:], rden[:], ALU.mult)
+            nc.sync.dma_start(out_blocks[cb, :, :], window[cb][:])

@@ -12,6 +12,8 @@ KB = K // P
 CB = C // P
 NEAR = 24.0
 D2_FLOOR = 1e-18
+BANK = 512
+WARM_MATMULS = 4
 FLOPS = 2 * D * K * N + 2 * K * C * N
 
 
@@ -41,6 +43,12 @@ def tile_nona_kernel(tc, x, x_neighbors, y, base, offs, out):
         nc.gpsimd.memset(ones[:], 1.0)
         near = held.tile([P, 1], F32, name="near")
         nc.gpsimd.memset(near[:], NEAR)
+
+        idle_in = held.tile([P, BANK], BF16, name="idle_in")
+        nc.vector.memset(idle_in[:], 0.0)
+        idle_out = psum.tile([P, BANK], F32, name="idle_out")
+        for i in range(WARM_MATMULS):
+            nc.tensor.matmul(idle_out[:], idle_in[:, :P], idle_in[:], start=True, stop=True)
 
         nb_sq = held.tile([P, K], BF16, name="nb_sq")
         nc.vector.tensor_tensor(nb_sq[:], nb_sb[:], nb_sb[:], ALU.mult)

@@ -11,9 +11,8 @@ D, K, C, S, N = 128, 256, 256, 256, 128
 KB = K // P
 CB = C // P
 NEAR = 24.0
-D2_FLOOR = 1e-18
-BANK = 512
-WARM_MATMULS = 4
+D2_FLOOR = 1e-30
+HUGE = 3.0e38
 FLOPS = 2 * D * K * N + 2 * K * C * N
 
 
@@ -44,12 +43,6 @@ def tile_nona_kernel(tc, x, x_neighbors, y, base, offs, out):
         near = held.tile([P, 1], F32, name="near")
         nc.gpsimd.memset(near[:], NEAR)
 
-        idle_in = held.tile([P, BANK], BF16, name="idle_in")
-        nc.vector.memset(idle_in[:], 0.0)
-        idle_out = psum.tile([P, BANK], F32, name="idle_out")
-        for i in range(WARM_MATMULS):
-            nc.tensor.matmul(idle_out[:], idle_in[:, :P], idle_in[:], start=True, stop=True)
-
         nb_sq = held.tile([P, K], BF16, name="nb_sq")
         nc.vector.tensor_tensor(nb_sq[:], nb_sb[:], nb_sb[:], ALU.mult)
         x_sq = held.tile([P, N], BF16, name="x_sq")
@@ -64,9 +57,11 @@ def tile_nona_kernel(tc, x, x_neighbors, y, base, offs, out):
         e = [held.tile([P, N], BF16, name=f"e{kb}") for kb in range(KB)]
         dist = [held.tile([P, N], F32, name=f"dist{kb}") for kb in range(KB)]
         for kb in range(KB):
-            d2 = held.tile([P, N], F32, name=f"d2_{kb}")
-            nc.vector.tensor_scalar(d2[:], neg_half_d2[kb][:], -2.0, D2_FLOOR, ALU.mult, ALU.max)
-            nc.scalar.activation(dist[kb][:], d2[:], ACT.Sqrt)
+            root = held.tile([P, N], F32, name=f"root{kb}")
+            nc.scalar.activation(root[:], neg_half_d2[kb][:], ACT.Sqrt, scale=-2.0)
+            cap = held.tile([P, N], F32, name=f"cap{kb}")
+            nc.vector.tensor_scalar(cap[:], neg_half_d2[kb][:], -0.5 * D2_FLOOR, HUGE, ALU.is_lt, ALU.mult)
+            nc.vector.scalar_tensor_tensor(dist[kb][:], root[:], 0.0, cap[:], ALU.max, ALU.min)
         for kb in range(KB):
             nc.scalar.activation(e[kb][:], dist[kb][:], ACT.Exp, bias=near[:], scale=-1.0)
 

@@ -37,11 +37,11 @@ def tile_nona_kernel(tc, x, x_neighbors, y, base, offs, out):
             nc.scalar.dma_start(window[cb][:], base_blocks[cb, :, :])
 
         neg_half = held.tile([P, P], BF16, name="neg_half")
-        nc.gpsimd.memset(neg_half[:], -0.5)
+        nc.vector.memset(neg_half[:], -0.5)
         ones = held.tile([P, P], BF16, name="ones")
-        nc.gpsimd.memset(ones[:], 1.0)
+        nc.vector.memset(ones[:], 1.0)
         near = held.tile([P, 1], F32, name="near")
-        nc.gpsimd.memset(near[:], NEAR)
+        nc.vector.memset(near[:], NEAR)
 
         nb_sq = held.tile([P, K], BF16, name="nb_sq")
         nc.vector.tensor_tensor(nb_sq[:], nb_sb[:], nb_sb[:], ALU.mult)

@@ -68,10 +68,12 @@ def tile_nona_kernel(tc, x, x_neighbors, y, base, offs, out):
         den = psum.tile([P, N], F32, name="den")
         num = [psum.tile([P, N], F32, name=f"num{cb}") for cb in range(CB)]
         for kb in range(KB):
-            first, last = kb == 0, kb == KB - 1
-            nc.tensor.matmul(den[:], ones[:], e[kb][:], start=first, stop=last)
-            for cb in range(CB):
-                nc.tensor.matmul(num[cb][:], y_sb[kb][:, cb * P : (cb + 1) * P], e[kb][:], start=first, stop=last)
+            nc.tensor.matmul(den[:], ones[:], e[kb][:], start=kb == 0, stop=kb == KB - 1)
+        for cb in range(CB):
+            for kb in range(KB):
+                nc.tensor.matmul(
+                    num[cb][:], y_sb[kb][:, cb * P : (cb + 1) * P], e[kb][:], start=kb == 0, stop=kb == KB - 1
+                )
         rden = held.tile([P, N], F32, name="rden")
         nc.vector.reciprocal(rden[:], den[:])
         num_sb = [held.tile([P, N], F32, name=f"num_sb{cb}") for cb in range(CB)]

@@ -10,6 +10,8 @@ P = 128
 D, K, C, S, N = 128, 256, 256, 256, 128
 KB = K // P
 CB = C // P
+QH = 2
+NH = N // QH
 NEAR = 24.0
 D2_FLOOR = 1e-30
 HUGE = 3.0e38
@@ -54,28 +56,33 @@ def tile_nona_kernel(tc, x, x_neighbors, y, base, offs, out):
             nc.tensor.matmul(neg_half_d2[kb][:], nb_sq[:, kb * P : (kb + 1) * P], neg_half[:], start=False, stop=False)
             nc.tensor.matmul(neg_half_d2[kb][:], neg_half[:], x_sq[:], start=False, stop=True)
 
-        e = [held.tile([P, N], BF16, name=f"e{kb}") for kb in range(KB)]
-        dist = [held.tile([P, N], F32, name=f"dist{kb}") for kb in range(KB)]
+        e = held.tile([P, KB, N], BF16, name="e")
+        dist = held.tile([P, KB, N], F32, name="dist")
         for kb in range(KB):
             root = held.tile([P, N], F32, name=f"root{kb}")
             nc.scalar.activation(root[:], neg_half_d2[kb][:], ACT.Sqrt, scale=-2.0)
             cap = held.tile([P, N], F32, name=f"cap{kb}")
             nc.vector.tensor_scalar(cap[:], neg_half_d2[kb][:], -0.5 * D2_FLOOR, HUGE, ALU.is_lt, ALU.mult)
-            nc.vector.scalar_tensor_tensor(dist[kb][:], root[:], 0.0, cap[:], ALU.max, ALU.min)
-        for kb in range(KB):
-            nc.scalar.activation(e[kb][:], dist[kb][:], ACT.Exp, bias=near[:], scale=-1.0)
+            nc.vector.scalar_tensor_tensor(dist[:, kb, :], root[:], 0.0, cap[:], ALU.max, ALU.min)
+        for qh in range(QH):
+            half = slice(qh * NH, (qh + 1) * NH)
+            nc.scalar.activation(e[:, :, half], dist[:, :, half], ACT.Exp, bias=near[:], scale=-1.0)
 
-        den = psum.tile([P, N], F32, name="den")
+        den = [psum.tile([P, NH], F32, name=f"den{qh}") for qh in range(QH)]
         num = [psum.tile([P, N], F32, name=f"num{cb}") for cb in range(CB)]
-        for kb in range(KB):
-            nc.tensor.matmul(den[:], ones[:], e[kb][:], start=kb == 0, stop=kb == KB - 1)
+        for qh in range(QH):
+            for kb in range(KB):
+                nc.tensor.matmul(
+                    den[qh][:], ones[:], e[:, kb, qh * NH : (qh + 1) * NH], start=kb == 0, stop=kb == KB - 1
+                )
         for cb in range(CB):
             for kb in range(KB):
                 nc.tensor.matmul(
-                    num[cb][:], y_sb[kb][:, cb * P : (cb + 1) * P], e[kb][:], start=kb == 0, stop=kb == KB - 1
+                    num[cb][:], y_sb[kb][:, cb * P : (cb + 1) * P], e[:, kb, :], start=kb == 0, stop=kb == KB - 1
                 )
         rden = held.tile([P, N], F32, name="rden")
-        nc.vector.reciprocal(rden[:], den[:])
+        for qh in range(QH):
+            nc.vector.reciprocal(rden[:, qh * NH : (qh + 1) * NH], den[qh][:])
         num_sb = [held.tile([P, N], F32, name=f"num_sb{cb}") for cb in range(CB)]
         for cb in range(CB):
             nc.scalar.copy(num_sb[cb][:], num[cb][:])

@@ -88,5 +88,8 @@ def tile_nona_kernel(tc, x, x_neighbors, y, base, offs, out):
             nc.scalar.copy(num_sb[cb][:], num[cb][:])
 
         for cb in range(CB):
-            nc.vector.tensor_tensor(window[cb][:].indirect(offsets[:]), num_sb[cb][:], rden[:], ALU.mult)
+            for qh in range(QH):
+                half = slice(qh * NH, (qh + 1) * NH)
+                places = offsets[:, qh * NH // 16 : (qh + 1) * NH // 16]
+                nc.vector.tensor_tensor(window[cb][:].indirect(places), num_sb[cb][:, half], rden[:, half], ALU.mult)
             nc.sync.dma_start(out_blocks[cb, :, :], window[cb][:])

@@ -46,9 +46,10 @@ def tile_nona_kernel(tc, x, x_neighbors, y, base, offs, out):
         nc.vector.memset(near[:], NEAR)
 
         nb_sq = held.tile([P, K], BF16, name="nb_sq")
-        nc.vector.tensor_tensor(nb_sq[:], nb_sb[:], nb_sb[:], ALU.mult)
         x_sq = held.tile([P, N], BF16, name="x_sq")
+        nc.vector.tensor_tensor(nb_sq[:, 0:P], nb_sb[:, 0:P], nb_sb[:, 0:P], ALU.mult)
         nc.vector.tensor_tensor(x_sq[:], x_sb[:], x_sb[:], ALU.mult)
+        nc.vector.tensor_tensor(nb_sq[:, P:K], nb_sb[:, P:K], nb_sb[:, P:K], ALU.mult)
         neg_half_d2 = [psum.tile([P, N], F32, name=f"neg_half_d2_{kb}") for kb in range(KB)]
         for kb in range(KB):
             nc.tensor.matmul(neg_half_d2[kb][:], nb_sb[:, kb * P : (kb + 1) * P], x_sb[:], start=True, stop=False)

@@ -12,6 +12,8 @@ KB = K // P
 CB = C // P
 QH = 2
 NH = N // QH
+QQ = 4
+NQ = N // QQ
 NEAR = 24.0
 D2_FLOOR = 1e-30
 HUGE = 3.0e38
@@ -65,16 +67,16 @@ def tile_nona_kernel(tc, x, x_neighbors, y, base, offs, out):
             cap = held.tile([P, N], F32, name=f"cap{kb}")
             nc.vector.tensor_scalar(cap[:], neg_half_d2[kb][:], -0.5 * D2_FLOOR, HUGE, ALU.is_lt, ALU.mult)
             nc.vector.scalar_tensor_tensor(dist[:, kb, :], root[:], 0.0, cap[:], ALU.max, ALU.min)
-        for qh in range(QH):
-            half = slice(qh * NH, (qh + 1) * NH)
-            nc.scalar.activation(e[:, :, half], dist[:, :, half], ACT.Exp, bias=near[:], scale=-1.0)
+        for qq in range(QQ):
+            quarter = slice(qq * NQ, (qq + 1) * NQ)
+            nc.scalar.activation(e[:, :, quarter], dist[:, :, quarter], ACT.Exp, bias=near[:], scale=-1.0)
 
-        den = [psum.tile([P, NH], F32, name=f"den{qh}") for qh in range(QH)]
+        den = [psum.tile([P, NQ], F32, name=f"den{qq}") for qq in range(QQ)]
         num = [psum.tile([P, N], F32, name=f"num{cb}") for cb in range(CB)]
-        for qh in range(QH):
+        for qq in range(QQ):
             for kb in range(KB):
                 nc.tensor.matmul(
-                    den[qh][:], ones[:], e[:, kb, qh * NH : (qh + 1) * NH], start=kb == 0, stop=kb == KB - 1
+                    den[qq][:], ones[:], e[:, kb, qq * NQ : (qq + 1) * NQ], start=kb == 0, stop=kb == KB - 1
                 )
         for cb in range(CB):
             for kb in range(KB):
@@ -82,8 +84,8 @@ def tile_nona_kernel(tc, x, x_neighbors, y, base, offs, out):
                     num[cb][:], y_sb[kb][:, cb * P : (cb + 1) * P], e[:, kb, :], start=kb == 0, stop=kb == KB - 1
                 )
         rden = held.tile([P, N], F32, name="rden")
-        for qh in range(QH):
-            nc.vector.reciprocal(rden[:, qh * NH : (qh + 1) * NH], den[qh][:])
+        for qq in range(QQ):
+            nc.vector.reciprocal(rden[:, qq * NQ : (qq + 1) * NQ], den[qq][:])
         num_sb = [held.tile([P, N], F32, name=f"num_sb{cb}") for cb in range(CB)]
         for cb in range(CB):
             nc.scalar.copy(num_sb[cb][:], num[cb][:])

@@ -38,7 +38,7 @@ def tile_nona_kernel(tc, x, x_neighbors, y, base, offs, out):
             nc.sync.dma_start(y_sb[kb][:], y_blocks[kb, :, :])
         window = [held.tile([P, S], F32, name=f"window{cb}") for cb in range(CB)]
         for cb in range(CB):
-            nc.scalar.dma_start(window[cb][:], base_blocks[cb, :, :])
+            nc.sync.dma_start(window[cb][:], base_blocks[cb, :, :])
 
         neg_half = held.tile([P, P], BF16, name="neg_half")
         nc.vector.memset(neg_half[:], -0.5)

@@ -88,7 +88,9 @@ def tile_nona_kernel(tc, x, x_neighbors, y, base, offs, out):
             nc.vector.reciprocal(rden[:, qq * NQ : (qq + 1) * NQ], den[qq][:])
         num_sb = [held.tile([P, N], F32, name=f"num_sb{cb}") for cb in range(CB)]
         for cb in range(CB):
-            nc.scalar.copy(num_sb[cb][:], num[cb][:])
+            for qh in range(QH):
+                half = slice(qh * NH, (qh + 1) * NH)
+                nc.scalar.copy(num_sb[cb][:, half], num[cb][:, half])
 
         for cb in range(CB):
             for qh in range(QH):

@@ -35,10 +35,10 @@ def tile_nona_kernel(tc, x, x_neighbors, y, base, offs, out):
         nc.sync.dma_start(offsets[:], offs)
         y_sb = [held.tile([P, C], BF16, name=f"y_sb{kb}") for kb in range(KB)]
         for kb in range(KB):
-            nc.sync.dma_start(y_sb[kb][:], y_blocks[kb, :, :])
+            nc.gpsimd.dma_start(y_sb[kb][:], y_blocks[kb, :, :])
         window = [held.tile([P, S], F32, name=f"window{cb}") for cb in range(CB)]
         for cb in range(CB):
-            nc.sync.dma_start(window[cb][:], base_blocks[cb, :, :])
+            nc.gpsimd.dma_start(window[cb][:], base_blocks[cb, :, :])
 
         neg_half = held.tile([P, P], BF16, name="neg_half")
         nc.vector.memset(neg_half[:], -0.5)

@@ -22,7 +22,7 @@ FLOPS = 2 * D * K * N + 2 * K * C * N
 
 def tile_nona_kernel(tc, x, x_neighbors, y, base, offs, out):
     nc = tc.nc
-    y_blocks = y.rearrange("(b p) c -> b p c", p=P)
+    y_blocks = y.rearrange("(b p) c -> p b c", p=P)
     base_blocks = base.rearrange("(b p) s -> b p s", p=P)
     out_blocks = out.rearrange("(b p) s -> b p s", p=P)
 
@@ -33,9 +33,8 @@ def tile_nona_kernel(tc, x, x_neighbors, y, base, offs, out):
         nc.scalar.dma_start(x_sb[:], x)
         offsets = held.tile([P, N // 16], U16, name="offsets")
         nc.sync.dma_start(offsets[:], offs)
-        y_sb = [held.tile([P, C], BF16, name=f"y_sb{kb}") for kb in range(KB)]
-        for kb in range(KB):
-            nc.gpsimd.dma_start(y_sb[kb][:], y_blocks[kb, :, :])
+        y_sb = held.tile([P, KB, C], BF16, name="y_sb")
+        nc.gpsimd.dma_start(y_sb[:], y_blocks)
         window = [held.tile([P, S], F32, name=f"window{cb}") for cb in range(CB)]
         for cb in range(CB):
             nc.gpsimd.dma_start(window[cb][:], base_blocks[cb, :, :])
@@ -81,7 +80,7 @@ def tile_nona_kernel(tc, x, x_neighbors, y, base, offs, out):
         for cb in range(CB):
             for kb in range(KB):
                 nc.tensor.matmul(
-                    num[cb][:], y_sb[kb][:, cb * P : (cb + 1) * P], e[:, kb, :], start=kb == 0, stop=kb == KB - 1
+                    num[cb][:], y_sb[:, kb, cb * P : (cb + 1) * P], e[:, kb, :], start=kb == 0, stop=kb == KB - 1
                 )
         rden = held.tile([P, N], F32, name="rden")
         for qq in range(QQ):

import concourse.mybir as mybir

BF16 = mybir.dt.bfloat16
F32 = mybir.dt.float32
U16 = mybir.dt.uint16
ACT = mybir.ActivationFunctionType
ALU = mybir.AluOpType

P = 128
D, K, C, S, N = 128, 256, 256, 256, 128
KB = K // P
CB = C // P
QH = 2
NH = N // QH
QQ = 4
NQ = N // QQ
NEAR = 24.0
D2_FLOOR = 1e-30
HUGE = 3.0e38
FLOPS = 2 * D * K * N + 2 * K * C * N


def tile_nona_kernel(tc, x, x_neighbors, y, base, offs, out):
    nc = tc.nc
    y_blocks = y.rearrange("(b p) c -> p b c", p=P)
    base_blocks = base.rearrange("(b p) s -> b p s", p=P)
    out_blocks = out.rearrange("(b p) s -> b p s", p=P)

    with tc.tile_pool(name="held", bufs=1) as held, tc.psum_pool(name="psum", bufs=1) as psum:
        nb_sb = held.tile([P, K], BF16, name="nb_sb")
        nc.sync.dma_start(nb_sb[:], x_neighbors)
        x_sb = held.tile([P, N], BF16, name="x_sb")
        nc.scalar.dma_start(x_sb[:], x)
        offsets = held.tile([P, N // 16], U16, name="offsets")
        nc.sync.dma_start(offsets[:], offs)
        y_sb = held.tile([P, KB, C], BF16, name="y_sb")
        nc.gpsimd.dma_start(y_sb[:], y_blocks)
        window = [held.tile([P, S], F32, name=f"window{cb}") for cb in range(CB)]
        for cb in range(CB):
            nc.gpsimd.dma_start(window[cb][:], base_blocks[cb, :, :])

        neg_half = held.tile([P, P], BF16, name="neg_half")
        nc.vector.memset(neg_half[:], -0.5)
        ones = held.tile([P, P], BF16, name="ones")
        nc.vector.memset(ones[:], 1.0)
        near = held.tile([P, 1], F32, name="near")
        nc.vector.memset(near[:], NEAR)

        nb_sq = held.tile([P, K], BF16, name="nb_sq")
        x_sq = held.tile([P, N], BF16, name="x_sq")
        nc.vector.tensor_tensor(nb_sq[:, 0:P], nb_sb[:, 0:P], nb_sb[:, 0:P], ALU.mult)
        nc.vector.tensor_tensor(x_sq[:], x_sb[:], x_sb[:], ALU.mult)
        nc.vector.tensor_tensor(nb_sq[:, P:K], nb_sb[:, P:K], nb_sb[:, P:K], ALU.mult)
        neg_half_d2 = [psum.tile([P, N], F32, name=f"neg_half_d2_{kb}") for kb in range(KB)]
        for kb in range(KB):
            nc.tensor.matmul(neg_half_d2[kb][:], nb_sb[:, kb * P : (kb + 1) * P], x_sb[:], start=True, stop=False)
        for kb in range(KB):
            nc.tensor.matmul(neg_half_d2[kb][:], nb_sq[:, kb * P : (kb + 1) * P], neg_half[:], start=False, stop=False)
            nc.tensor.matmul(neg_half_d2[kb][:], neg_half[:], x_sq[:], start=False, stop=True)

        e = held.tile([P, KB, N], BF16, name="e")
        dist = held.tile([P, KB, N], F32, name="dist")
        for kb in range(KB):
            root = held.tile([P, N], F32, name=f"root{kb}")
            nc.scalar.activation(root[:], neg_half_d2[kb][:], ACT.Sqrt, scale=-2.0)
            cap = held.tile([P, N], F32, name=f"cap{kb}")
            nc.vector.tensor_scalar(cap[:], neg_half_d2[kb][:], -0.5 * D2_FLOOR, HUGE, ALU.is_lt, ALU.mult)
            nc.vector.scalar_tensor_tensor(dist[:, kb, :], root[:], 0.0, cap[:], ALU.max, ALU.min)
        for qq in range(QQ):
            quarter = slice(qq * NQ, (qq + 1) * NQ)
            nc.scalar.activation(e[:, :, quarter], dist[:, :, quarter], ACT.Exp, bias=near[:], scale=-1.0)

        den = [psum.tile([P, NQ], F32, name=f"den{qq}") for qq in range(QQ)]
        num = [psum.tile([P, N], F32, name=f"num{cb}") for cb in range(CB)]
        for qq in range(QQ):
            for kb in range(KB):
                nc.tensor.matmul(
                    den[qq][:], ones[:], e[:, kb, qq * NQ : (qq + 1) * NQ], start=kb == 0, stop=kb == KB - 1
                )
        for cb in range(CB):
            for kb in range(KB):
                nc.tensor.matmul(
                    num[cb][:], y_sb[:, kb, cb * P : (cb + 1) * P], e[:, kb, :], start=kb == 0, stop=kb == KB - 1
                )
        rden = held.tile([P, N], F32, name="rden")
        for qq in range(QQ):
            nc.vector.reciprocal(rden[:, qq * NQ : (qq + 1) * NQ], den[qq][:])
        num_sb = [held.tile([P, N], F32, name=f"num_sb{cb}") for cb in range(CB)]
        for cb in range(CB):
            for qh in range(QH):
                half = slice(qh * NH, (qh + 1) * NH)
                nc.scalar.copy(num_sb[cb][:, half], num[cb][:, half])

        for cb in range(CB):
            for qh in range(QH):
                half = slice(qh * NH, (qh + 1) * NH)
                places = offsets[:, qh * NH // 16 : (qh + 1) * NH // 16]
                nc.vector.tensor_tensor(window[cb][:].indirect(places), num_sb[cb][:, half], rden[:, half], ALU.mult)
            nc.sync.dma_start(out_blocks[cb, :, :], window[cb][:])
